import numpy as np
import ml_dtypes


def mxq(x, axis, fmt="e4m3"):
    dtype, down = {"e4m3": (ml_dtypes.float8_e4m3fn, 7), "e5m2": (ml_dtypes.float8_e5m2, 14)}[fmt]
    v = np.moveaxis(np.asarray(x, np.float32).astype(ml_dtypes.bfloat16).astype(np.float64), axis, -1)
    blocks = v.reshape(v.shape[:-1] + (-1, 32))
    amax = np.abs(blocks).max(-1, keepdims=True)
    byte = np.maximum(np.where(amax > 0, np.frexp(amax)[1] - 1 + 127, 0) - down, 1)
    scale = np.exp2(byte - 127.0)
    codes = (blocks / scale).astype(np.float32).astype(dtype).astype(np.float64)
    return np.moveaxis((codes * scale).reshape(v.shape), -1, axis)


WIDE = False


def mx_kscale(k):
    if not WIDE:
        return np.ones(k)
    levels = np.array([10, -10, 5, -5, 0])
    a = np.random.permutation(np.resize(levels, k // 512 * 4)).reshape(k // 512, 4)
    idx = np.arange(k)
    return np.exp2(a[idx // 512, idx % 128 // 32])


BF16 = ml_dtypes.bfloat16


def bf(x):
    return np.asarray(x, np.float32).astype(BF16)


def f64(x):
    return np.asarray(x).astype(np.float64)


B, T, C, H = 4, 128, 2048, 32
HD = C // H


def rotary_pos_emb(v):
    exponents = f64(np.arange(0, HD, 2)[: HD // 2] // HD)
    freqs = 1.0 / np.power(1000.0, exponents)
    theta = f64(np.arange(T))[:, None] * freqs[None, :]
    cos = np.cos(theta)[None, :, None, :]
    sin = np.sin(theta)[None, :, None, :]
    vr = v.reshape(B, T, H, HD // 2, 2)
    v0, v1 = vr[..., 0], vr[..., 1]
    out = np.stack([v0 * cos - v1 * sin, v0 * sin + v1 * cos], axis=-1)
    return out.reshape(B, T, H, HD)


def setup_inputs():
    s = mx_kscale(C)
    return {"x": bf(np.random.standard_normal((B, T, C)) * s),
            "wq": bf(np.random.standard_normal((C, C)) / np.sqrt(C) / s[None, :]),
            "wk": bf(np.random.standard_normal((C, C)) / np.sqrt(C) / s[None, :])}


def reference(x, wq, wk):
    xm = mxq(f64(x), 2, "e4m3")
    q = (xm @ mxq(f64(wq), 1, "e4m3").T).reshape(B, T, H, HD)
    k = (xm @ mxq(f64(wk), 1, "e4m3").T).reshape(B, T, H, HD)
    return rotary_pos_emb(q), rotary_pos_emb(k)

@@ -1,0 +1,197 @@
+import math
+from contextlib import ExitStack
+
+import concourse.mybir as mybir
+from concourse.masks import make_identity
+
+F32 = mybir.dt.float32
+BF16 = mybir.dt.bfloat16
+I32 = mybir.dt.int32
+U32 = mybir.dt.uint32
+U8 = mybir.dt.uint8
+FP8X4 = mybir.dt.float8_e4m3fn_x4
+ALU = mybir.AluOpType
+ACT = mybir.ActivationFunctionType
+
+P = 128
+BATCHES = 4
+CHANNELS = 2048
+PACK = 4
+PASSES = CHANNELS // (P * PACK)
+GROUP_ROWS = 512
+HALF_ROWS = GROUP_ROWS // 2
+BLOCKS = GROUP_ROWS // P
+GROUPS_PER_WEIGHT = CHANNELS // GROUP_ROWS
+WEIGHT_GROUPS = 2 * GROUPS_PER_WEIGHT
+LOADS_AHEAD = 4
+
+FLOPS = 2 * (BATCHES * P) * CHANNELS * (2 * CHANNELS)
+
+TWO_PI = 2.0 * math.pi
+TWO_PI_HIGH = 6.28125
+TWO_PI_MID = int((TWO_PI - TWO_PI_HIGH) * 2**25) / 2**25
+TWO_PI_LOW = TWO_PI - TWO_PI_HIGH - TWO_PI_MID
+HALF_PI_HIGH = int(0.5 * math.pi * 2**20) / 2**20
+HALF_PI_LOW = 0.5 * math.pi - HALF_PI_HIGH
+ROUND_TO_WHOLE = 1.5 * 2**23
+
+
+def position_trig(nc, pool):
+    position_int = pool.tile([P, 1], I32, name="position_int")
+    nc.gpsimd.iota(position_int[:], pattern=[[0, 1]], base=0, channel_multiplier=1)
+    position = pool.tile([P, 1], F32, name="position")
+    nc.vector.tensor_copy(out=position[:], in_=position_int[:])
+
+    shifted = pool.tile([P, 1], F32, name="shifted")
+    nc.vector.tensor_scalar(
+        out=shifted[:], in0=position[:], scalar1=1.0 / TWO_PI, scalar2=ROUND_TO_WHOLE, op0=ALU.mult, op1=ALU.add
+    )
+    turns = pool.tile([P, 1], F32, name="turns")
+    nc.vector.tensor_scalar(out=turns[:], in0=shifted[:], scalar1=ROUND_TO_WHOLE, scalar2=None, op0=ALU.subtract)
+
+    angles = pool.tile([P, 2], F32, name="angles")
+    less_high = pool.tile([P, 1], F32, name="less_high")
+    less_mid = pool.tile([P, 1], F32, name="less_mid")
+    nc.vector.scalar_tensor_tensor(
+        out=less_high[:], in0=turns[:], scalar=-TWO_PI_HIGH, in1=position[:], op0=ALU.mult, op1=ALU.add
+    )
+    nc.vector.scalar_tensor_tensor(
+        out=less_mid[:], in0=turns[:], scalar=-TWO_PI_MID, in1=less_high[:], op0=ALU.mult, op1=ALU.add
+    )
+    nc.vector.scalar_tensor_tensor(
+        out=angles[:, 0:1], in0=turns[:], scalar=-TWO_PI_LOW, in1=less_mid[:], op0=ALU.mult, op1=ALU.add
+    )
+    magnitude = pool.tile([P, 1], F32, name="magnitude")
+    nc.vector.scalar_tensor_tensor(
+        out=magnitude[:], in0=angles[:, 0:1], scalar=-1.0, in1=angles[:, 0:1], op0=ALU.mult, op1=ALU.max
+    )
+    nc.vector.tensor_scalar(
+        out=angles[:, 1:2],
+        in0=magnitude[:],
+        scalar1=HALF_PI_HIGH,
+        scalar2=HALF_PI_LOW,
+        op0=ALU.subtract,
+        op1=ALU.subtract,
+    )
+
+    sines = pool.tile([P, 2], F32, name="sines")
+    nc.scalar.activation(out=sines[:], in_=angles[:], func=ACT.Sin)
+    negated = pool.tile([P, 2], F32, name="negated")
+    nc.vector.tensor_scalar(out=negated[:], in0=sines[:], scalar1=-1.0, scalar2=None, op0=ALU.mult)
+    return sines[:, 0:1], negated[:, 0:1], negated[:, 1:2]
+
+
+def tile_attention_pa_kernel(tc, x, wq, wk, out_0, out_1):
+    nc = tc.nc
+
+    group_halves = [[x[2 * half : 2 * half + 2].rearrange("b t k -> t b k") for half in range(2)]]
+    for weight in (wq, wk):
+        for c in range(GROUPS_PER_WEIGHT):
+            rows = weight[c * GROUP_ROWS : (c + 1) * GROUP_ROWS, :]
+            by_parity = rows.rearrange("(h r two) k -> two r h k", h=2, two=2)
+            group_halves.append([by_parity[two] for two in range(2)])
+
+    outputs = [out.rearrange("b t h d -> b t (h d)") for out in (out_0, out_1)]
+
+    with ExitStack() as stack:
+        const = stack.enter_context(tc.tile_pool(name="const", bufs=1))
+        raw_pool = stack.enter_context(tc.tile_pool(name="raw", bufs=LOADS_AHEAD + 1))
+        grouped_pool = stack.enter_context(tc.tile_pool(name="grouped", bufs=2 * PASSES))
+        weight_mx = stack.enter_context(tc.tile_pool(name="weight_mx", bufs=3))
+        crossed_pool = stack.enter_context(tc.tile_pool(name="crossed", bufs=4))
+        rotated_pool = stack.enter_context(tc.tile_pool(name="rotated", bufs=6))
+        transposed_pool = stack.enter_context(tc.psum_pool(name="transposed", bufs=4))
+        acc_pool = stack.enter_context(tc.psum_pool(name="acc", bufs=4))
+        stack.enter_context(tc.manual_schedule())
+
+        raw_tiles = {}
+
+        def start_load(n):
+            raw = raw_pool.tile([P, BLOCKS, CHANNELS], BF16, name="raw")
+            for half in range(2):
+                nc.sync.dma_start(out=raw[:, 2 * half : 2 * half + 2, :], in_=group_halves[n][half])
+            raw_tiles[n] = raw
+
+        def quantise_half(n, half, codes, scales):
+            raw_words = raw_tiles[n][:].bitcast(F32)
+            columns = slice(half * HALF_ROWS, (half + 1) * HALF_ROWS)
+            grouped_tiles = []
+            for g in range(PASSES):
+                bank = transposed_pool.tile([P, 2, 2, P], F32, name="bank")
+                for u in range(2):
+                    first_word = (2 * g + u) * P
+                    for j in range(2):
+                        nc.tensor.transpose(
+                            out=bank[:, u, j, :],
+                            in_=raw_words[:, 2 * half + j, first_word : first_word + P],
+                            identity=identity[:],
+                        )
+                grouped = grouped_pool.tile([P, HALF_ROWS, PACK], BF16, name="grouped", align_bytes=64)
+                copy_out = nc.vector.tensor_copy if g == PASSES - 1 else nc.scalar.copy
+                copy_out(out=grouped[:].bitcast(F32), in_=bank[:].rearrange("p u j r -> p (j r) u"))
+                grouped_tiles.append(grouped)
+            for g in range(PASSES):
+                nc.vector.quantize_mx(
+                    out=codes[:, g, columns].bitcast(FP8X4),
+                    scales=scales[:, g, columns],
+                    in_=grouped_tiles[g][:].rearrange("p n t -> p (n t)"),
+                )
+
+        def project_and_rotate(c, b, w_codes, w_scales):
+            tokens = slice(b * P, (b + 1) * P)
+            acc = acc_pool.tile([P, GROUP_ROWS], F32, name="acc")
+            for g in range(PASSES):
+                nc.tensor.matmul_mx(
+                    out=acc[:],
+                    lhsT=x_codes[:, g, tokens].bitcast(FP8X4),
+                    lhsT_scale=x_scales[:, g, tokens],
+                    rhs=w_codes[:, g, :].bitcast(FP8X4),
+                    rhs_scale=w_scales[:, g, :],
+                    start=(g == 0),
+                    stop=(g == PASSES - 1),
+                )
+            crossed = crossed_pool.tile([P, GROUP_ROWS], F32, name="crossed")
+            nc.scalar.activation(out=crossed[:, :HALF_ROWS], in_=acc[:, HALF_ROWS:], func=ACT.Copy, scale=minus_sin_t)
+            nc.scalar.activation(out=crossed[:, HALF_ROWS:], in_=acc[:, :HALF_ROWS], func=ACT.Copy, scale=sin_t)
+            rotated = rotated_pool.tile([P, HALF_ROWS, 2], F32, name="rotated")
+            nc.vector.scalar_tensor_tensor(
+                out=rotated[:],
+                in0=acc[:].rearrange("p (two i) -> p i two", two=2),
+                scalar=cos_t,
+                in1=crossed[:].rearrange("p (two i) -> p i two", two=2),
+                op0=ALU.mult,
+                op1=ALU.add,
+            )
+            first_channel = (c % GROUPS_PER_WEIGHT) * GROUP_ROWS
+            nc.sync.dma_start(
+                out=outputs[c // GROUPS_PER_WEIGHT][b, :, first_channel : first_channel + GROUP_ROWS],
+                in_=rotated[:].rearrange("p i two -> p (i two)"),
+            )
+
+        for n in range(LOADS_AHEAD):
+            start_load(n)
+
+        identity = const.tile([P, P], F32, name="identity")
+        make_identity(nc, identity[:])
+
+        sin_t, minus_sin_t, cos_t = position_trig(nc, const)
+
+        x_codes = const.tile([P, PASSES, GROUP_ROWS], U32, name="x_codes", align_bytes=64)
+        x_scales = const.tile([P, PASSES, GROUP_ROWS], U8, name="x_scales", align_bytes=64)
+        for half in range(2):
+            quantise_half(0, half, x_codes, x_scales)
+
+        prepared = {}
+        for c in range(WEIGHT_GROUPS + 1):
+            if c + LOADS_AHEAD <= WEIGHT_GROUPS:
+                start_load(c + LOADS_AHEAD)
+            if c < WEIGHT_GROUPS:
+                w_codes = weight_mx.tile([P, PASSES, GROUP_ROWS], U32, name="w_codes", align_bytes=64)
+                w_scales = weight_mx.tile([P, PASSES, GROUP_ROWS], U8, name="w_scales", align_bytes=64)
+                prepared[c] = (w_codes, w_scales)
+            for half in range(2):
+                if c < WEIGHT_GROUPS:
+                    quantise_half(c + 1, half, prepared[c][0], prepared[c][1])
+                if c > 0:
+                    for b in (2 * half, 2 * half + 1):
+                        project_and_rotate(c - 1, b, prepared[c - 1][0], prepared[c - 1][1])

@@ -18,12 +18,17 @@ BATCHES = 4
 CHANNELS = 2048
 PACK = 4
 PASSES = CHANNELS // (P * PACK)
-GROUP_ROWS = 512
-HALF_ROWS = GROUP_ROWS // 2
-BLOCKS = GROUP_ROWS // P
-GROUPS_PER_WEIGHT = CHANNELS // GROUP_ROWS
-WEIGHT_GROUPS = 2 * GROUPS_PER_WEIGHT
-LOADS_AHEAD = 4
+UNIT_ROWS = 2 * P
+X_UNITS = BATCHES * P // UNIT_ROWS
+UNITS_PER_WEIGHT = CHANNELS // UNIT_ROWS
+WEIGHT_UNITS = 2 * UNITS_PER_WEIGHT
+UNITS_PER_ROUND = 2
+ROUNDS = WEIGHT_UNITS // UNITS_PER_ROUND
+LAG = 1
+LOADS_AHEAD = 8
+RAW_BUFFERS = LOADS_AHEAD + 2
+TRANSPOSE_BANKS = 5
+ACCUMULATOR_BANKS = 3
 
 FLOPS = 2 * (BATCHES * P) * CHANNELS * (2 * CHANNELS)
 
@@ -84,89 +89,95 @@ def position_trig(nc, pool):
 def tile_attention_pa_kernel(tc, x, wq, wk, out_0, out_1):
     nc = tc.nc
 
-    group_halves = [[x[2 * half : 2 * half + 2].rearrange("b t k -> t b k") for half in range(2)]]
+    sources = [x[2 * h : 2 * h + 2].rearrange("b t k -> t b k") for h in range(X_UNITS)]
     for weight in (wq, wk):
-        for c in range(GROUPS_PER_WEIGHT):
-            rows = weight[c * GROUP_ROWS : (c + 1) * GROUP_ROWS, :]
-            by_parity = rows.rearrange("(h r two) k -> two r h k", h=2, two=2)
-            group_halves.append([by_parity[two] for two in range(2)])
+        for c in range(UNITS_PER_WEIGHT):
+            rows = weight[c * UNIT_ROWS : (c + 1) * UNIT_ROWS, :]
+            sources.append(rows.rearrange("(r parity) k -> r parity k", parity=2))
 
     outputs = [out.rearrange("b t h d -> b t (h d)") for out in (out_0, out_1)]
 
     with ExitStack() as stack:
         const = stack.enter_context(tc.tile_pool(name="const", bufs=1))
-        raw_pool = stack.enter_context(tc.tile_pool(name="raw", bufs=LOADS_AHEAD + 1))
-        grouped_pool = stack.enter_context(tc.tile_pool(name="grouped", bufs=2 * PASSES))
-        weight_mx = stack.enter_context(tc.tile_pool(name="weight_mx", bufs=3))
-        crossed_pool = stack.enter_context(tc.tile_pool(name="crossed", bufs=4))
-        rotated_pool = stack.enter_context(tc.tile_pool(name="rotated", bufs=6))
-        transposed_pool = stack.enter_context(tc.psum_pool(name="transposed", bufs=4))
-        acc_pool = stack.enter_context(tc.psum_pool(name="acc", bufs=4))
+        raw_pool = stack.enter_context(tc.tile_pool(name="raw", bufs=RAW_BUFFERS))
+        grouped_pool = stack.enter_context(tc.tile_pool(name="grouped", bufs=UNITS_PER_ROUND * PASSES))
+        weight_mx = stack.enter_context(tc.tile_pool(name="weight_mx", bufs=2 * UNITS_PER_ROUND))
+        crossed_pool = stack.enter_context(tc.tile_pool(name="crossed", bufs=ACCUMULATOR_BANKS))
+        rotated_pool = stack.enter_context(tc.tile_pool(name="rotated", bufs=2 * ACCUMULATOR_BANKS))
+        transposed_pool = stack.enter_context(tc.psum_pool(name="transposed", bufs=TRANSPOSE_BANKS))
+        acc_pool = stack.enter_context(tc.psum_pool(name="acc", bufs=ACCUMULATOR_BANKS))
         stack.enter_context(tc.manual_schedule())
 
         raw_tiles = {}
 
         def start_load(n):
-            raw = raw_pool.tile([P, BLOCKS, CHANNELS], BF16, name="raw")
-            for half in range(2):
-                nc.sync.dma_start(out=raw[:, 2 * half : 2 * half + 2, :], in_=group_halves[n][half])
+            raw = raw_pool.tile([P, 2, CHANNELS], BF16, name="raw")
+            nc.sync.dma_start(out=raw[:], in_=sources[n])
             raw_tiles[n] = raw
 
-        def quantise_half(n, half, codes, scales):
+        def transpose_and_quantise(n, codes, scales):
+            if n + LOADS_AHEAD < len(sources):
+                start_load(n + LOADS_AHEAD)
             raw_words = raw_tiles[n][:].bitcast(F32)
-            columns = slice(half * HALF_ROWS, (half + 1) * HALF_ROWS)
             grouped_tiles = []
             for g in range(PASSES):
                 bank = transposed_pool.tile([P, 2, 2, P], F32, name="bank")
-                for u in range(2):
-                    first_word = (2 * g + u) * P
+                for plane in range(2):
+                    first_word = (2 * g + plane) * P
                     for j in range(2):
                         nc.tensor.transpose(
-                            out=bank[:, u, j, :],
-                            in_=raw_words[:, 2 * half + j, first_word : first_word + P],
+                            out=bank[:, plane, j, :],
+                            in_=raw_words[:, j, first_word : first_word + P],
                             identity=identity[:],
                         )
-                grouped = grouped_pool.tile([P, HALF_ROWS, PACK], BF16, name="grouped", align_bytes=64)
+                grouped = grouped_pool.tile([P, UNIT_ROWS, PACK], BF16, name="grouped", align_bytes=64)
                 copy_out = nc.vector.tensor_copy if g == PASSES - 1 else nc.scalar.copy
-                copy_out(out=grouped[:].bitcast(F32), in_=bank[:].rearrange("p u j r -> p (j r) u"))
+                copy_out(out=grouped[:].bitcast(F32), in_=bank[:].rearrange("p plane j r -> p (j r) plane"))
                 grouped_tiles.append(grouped)
             for g in range(PASSES):
                 nc.vector.quantize_mx(
-                    out=codes[:, g, columns].bitcast(FP8X4),
-                    scales=scales[:, g, columns],
+                    out=codes[:, g, :].bitcast(FP8X4),
+                    scales=scales[:, g, :],
                     in_=grouped_tiles[g][:].rearrange("p n t -> p (n t)"),
                 )
 
-        def project_and_rotate(c, b, w_codes, w_scales):
-            tokens = slice(b * P, (b + 1) * P)
-            acc = acc_pool.tile([P, GROUP_ROWS], F32, name="acc")
-            for g in range(PASSES):
-                nc.tensor.matmul_mx(
-                    out=acc[:],
-                    lhsT=x_codes[:, g, tokens].bitcast(FP8X4),
-                    lhsT_scale=x_scales[:, g, tokens],
-                    rhs=w_codes[:, g, :].bitcast(FP8X4),
-                    rhs_scale=w_scales[:, g, :],
-                    start=(g == 0),
-                    stop=(g == PASSES - 1),
+        def project_and_rotate(unit):
+            w_codes, w_scales = prepared[unit]
+            result = outputs[unit // UNITS_PER_WEIGHT]
+            first_channel = (unit % UNITS_PER_WEIGHT) * UNIT_ROWS
+            for first_batch in range(0, BATCHES, 2):
+                acc = acc_pool.tile([P, 2, 2, P], F32, name="acc")
+                for j in range(2):
+                    tokens = slice((first_batch + j) * P, (first_batch + j + 1) * P)
+                    for g in range(PASSES):
+                        nc.tensor.matmul_mx(
+                            out=acc[:, j, :, :].rearrange("p parity i -> p (parity i)"),
+                            lhsT=x_codes[:, g, tokens].bitcast(FP8X4),
+                            lhsT_scale=x_scales[:, g, tokens],
+                            rhs=w_codes[:, g, :].bitcast(FP8X4),
+                            rhs_scale=w_scales[:, g, :],
+                            start=(g == 0),
+                            stop=(g == PASSES - 1),
+                        )
+                crossed = crossed_pool.tile([P, 2, 2, P], F32, name="crossed")
+                nc.scalar.activation(out=crossed[:, :, 0, :], in_=acc[:, :, 1, :], func=ACT.Copy, scale=minus_sin_t)
+                nc.scalar.activation(out=crossed[:, :, 1, :], in_=acc[:, :, 0, :], func=ACT.Copy, scale=sin_t)
+                rotated = rotated_pool.tile([P, 2, P, 2], F32, name="rotated")
+                for j in range(2):
+                    nc.vector.scalar_tensor_tensor(
+                        out=rotated[:, j, :, :],
+                        in0=acc[:, j, :, :].rearrange("p parity i -> p i parity"),
+                        scalar=cos_t,
+                        in1=crossed[:, j, :, :].rearrange("p parity i -> p i parity"),
+                        op0=ALU.mult,
+                        op1=ALU.add,
+                    )
+                nc.sync.dma_start(
+                    out=result[first_batch : first_batch + 2, :, first_channel : first_channel + UNIT_ROWS].rearrange(
+                        "b t c -> t b c"
+                    ),
+                    in_=rotated[:].rearrange("p j i parity -> p j (i parity)"),
                 )
-            crossed = crossed_pool.tile([P, GROUP_ROWS], F32, name="crossed")
-            nc.scalar.activation(out=crossed[:, :HALF_ROWS], in_=acc[:, HALF_ROWS:], func=ACT.Copy, scale=minus_sin_t)
-            nc.scalar.activation(out=crossed[:, HALF_ROWS:], in_=acc[:, :HALF_ROWS], func=ACT.Copy, scale=sin_t)
-            rotated = rotated_pool.tile([P, HALF_ROWS, 2], F32, name="rotated")
-            nc.vector.scalar_tensor_tensor(
-                out=rotated[:],
-                in0=acc[:].rearrange("p (two i) -> p i two", two=2),
-                scalar=cos_t,
-                in1=crossed[:].rearrange("p (two i) -> p i two", two=2),
-                op0=ALU.mult,
-                op1=ALU.add,
-            )
-            first_channel = (c % GROUPS_PER_WEIGHT) * GROUP_ROWS
-            nc.sync.dma_start(
-                out=outputs[c // GROUPS_PER_WEIGHT][b, :, first_channel : first_channel + GROUP_ROWS],
-                in_=rotated[:].rearrange("p i two -> p (i two)"),
-            )
 
         for n in range(LOADS_AHEAD):
             start_load(n)
@@ -176,22 +187,18 @@ def tile_attention_pa_kernel(tc, x, wq, wk, out_0, out_1):
 
         sin_t, minus_sin_t, cos_t = position_trig(nc, const)
 
-        x_codes = const.tile([P, PASSES, GROUP_ROWS], U32, name="x_codes", align_bytes=64)
-        x_scales = const.tile([P, PASSES, GROUP_ROWS], U8, name="x_scales", align_bytes=64)
-        for half in range(2):
-            quantise_half(0, half, x_codes, x_scales)
+        x_codes = const.tile([P, PASSES, BATCHES * P], U32, name="x_codes", align_bytes=64)
+        x_scales = const.tile([P, PASSES, BATCHES * P], U8, name="x_scales", align_bytes=64)
+        for h in range(X_UNITS):
+            tokens_of_unit = slice(h * UNIT_ROWS, (h + 1) * UNIT_ROWS)
+            transpose_and_quantise(h, x_codes[:, :, tokens_of_unit], x_scales[:, :, tokens_of_unit])
 
         prepared = {}
-        for c in range(WEIGHT_GROUPS + 1):
-            if c + LOADS_AHEAD <= WEIGHT_GROUPS:
-                start_load(c + LOADS_AHEAD)
-            if c < WEIGHT_GROUPS:
-                w_codes = weight_mx.tile([P, PASSES, GROUP_ROWS], U32, name="w_codes", align_bytes=64)
-                w_scales = weight_mx.tile([P, PASSES, GROUP_ROWS], U8, name="w_scales", align_bytes=64)
-                prepared[c] = (w_codes, w_scales)
-            for half in range(2):
-                if c < WEIGHT_GROUPS:
-                    quantise_half(c + 1, half, prepared[c][0], prepared[c][1])
-                if c > 0:
-                    for b in (2 * half, 2 * half + 1):
-                        project_and_rotate(c - 1, b, prepared[c - 1][0], prepared[c - 1][1])
+        for r in range(ROUNDS + 1):
+            for unit in range(UNITS_PER_ROUND * r, min(UNITS_PER_ROUND * (r + 1), WEIGHT_UNITS)):
+                w_codes = weight_mx.tile([P, PASSES, UNIT_ROWS], U32, name="w_codes", align_bytes=64)
+                w_scales = weight_mx.tile([P, PASSES, UNIT_ROWS], U8, name="w_scales", align_bytes=64)
+                prepared[unit] = (w_codes, w_scales)
+                transpose_and_quantise(X_UNITS + unit, w_codes, w_scales)
+            for unit in range(max(UNITS_PER_ROUND * r - LAG, 0), min(UNITS_PER_ROUND * (r + 1) - LAG, WEIGHT_UNITS)):
+                project_and_rotate(unit)

@@ -22,13 +22,10 @@ UNIT_ROWS = 2 * P
 X_UNITS = BATCHES * P // UNIT_ROWS
 UNITS_PER_WEIGHT = CHANNELS // UNIT_ROWS
 WEIGHT_UNITS = 2 * UNITS_PER_WEIGHT
-UNITS_PER_ROUND = 2
-ROUNDS = WEIGHT_UNITS // UNITS_PER_ROUND
-LAG = 1
 LOADS_AHEAD = 8
 RAW_BUFFERS = LOADS_AHEAD + 2
-TRANSPOSE_BANKS = 5
-ACCUMULATOR_BANKS = 3
+TRANSPOSE_BANKS = 4
+ACCUMULATOR_BANKS = 4
 
 FLOPS = 2 * (BATCHES * P) * CHANNELS * (2 * CHANNELS)
 
@@ -93,17 +90,17 @@ def tile_attention_pa_kernel(tc, x, wq, wk, out_0, out_1):
     for weight in (wq, wk):
         for c in range(UNITS_PER_WEIGHT):
             rows = weight[c * UNIT_ROWS : (c + 1) * UNIT_ROWS, :]
-            sources.append(rows.rearrange("(r parity) k -> r parity k", parity=2))
+            sources.append(rows.rearrange("(j r) k -> r j k", j=2))
 
     outputs = [out.rearrange("b t h d -> b t (h d)") for out in (out_0, out_1)]
 
     with ExitStack() as stack:
         const = stack.enter_context(tc.tile_pool(name="const", bufs=1))
         raw_pool = stack.enter_context(tc.tile_pool(name="raw", bufs=RAW_BUFFERS))
-        grouped_pool = stack.enter_context(tc.tile_pool(name="grouped", bufs=UNITS_PER_ROUND * PASSES))
-        weight_mx = stack.enter_context(tc.tile_pool(name="weight_mx", bufs=2 * UNITS_PER_ROUND))
+        grouped_pool = stack.enter_context(tc.tile_pool(name="grouped", bufs=2 * PASSES))
+        weight_mx = stack.enter_context(tc.tile_pool(name="weight_mx", bufs=3))
         crossed_pool = stack.enter_context(tc.tile_pool(name="crossed", bufs=ACCUMULATOR_BANKS))
-        rotated_pool = stack.enter_context(tc.tile_pool(name="rotated", bufs=2 * ACCUMULATOR_BANKS))
+        rotated_pool = stack.enter_context(tc.tile_pool(name="rotated", bufs=ACCUMULATOR_BANKS + 2))
         transposed_pool = stack.enter_context(tc.psum_pool(name="transposed", bufs=TRANSPOSE_BANKS))
         acc_pool = stack.enter_context(tc.psum_pool(name="acc", bufs=ACCUMULATOR_BANKS))
         stack.enter_context(tc.manual_schedule())
@@ -146,12 +143,12 @@ def tile_attention_pa_kernel(tc, x, wq, wk, out_0, out_1):
             result = outputs[unit // UNITS_PER_WEIGHT]
             first_channel = (unit % UNITS_PER_WEIGHT) * UNIT_ROWS
             for first_batch in range(0, BATCHES, 2):
-                acc = acc_pool.tile([P, 2, 2, P], F32, name="acc")
+                acc = acc_pool.tile([P, 2, UNIT_ROWS], F32, name="acc")
                 for j in range(2):
                     tokens = slice((first_batch + j) * P, (first_batch + j + 1) * P)
                     for g in range(PASSES):
                         nc.tensor.matmul_mx(
-                            out=acc[:, j, :, :].rearrange("p parity i -> p (parity i)"),
+                            out=acc[:, j, :],
                             lhsT=x_codes[:, g, tokens].bitcast(FP8X4),
                             lhsT_scale=x_scales[:, g, tokens],
                             rhs=w_codes[:, g, :].bitcast(FP8X4),
@@ -159,24 +156,24 @@ def tile_attention_pa_kernel(tc, x, wq, wk, out_0, out_1):
                             start=(g == 0),
                             stop=(g == PASSES - 1),
                         )
-                crossed = crossed_pool.tile([P, 2, 2, P], F32, name="crossed")
-                nc.scalar.activation(out=crossed[:, :, 0, :], in_=acc[:, :, 1, :], func=ACT.Copy, scale=minus_sin_t)
-                nc.scalar.activation(out=crossed[:, :, 1, :], in_=acc[:, :, 0, :], func=ACT.Copy, scale=sin_t)
-                rotated = rotated_pool.tile([P, 2, P, 2], F32, name="rotated")
-                for j in range(2):
-                    nc.vector.scalar_tensor_tensor(
-                        out=rotated[:, j, :, :],
-                        in0=acc[:, j, :, :].rearrange("p parity i -> p i parity"),
-                        scalar=cos_t,
-                        in1=crossed[:, j, :, :].rearrange("p parity i -> p i parity"),
-                        op0=ALU.mult,
-                        op1=ALU.add,
-                    )
+                pairs = acc[:].rearrange("p j (i parity) -> p (j i) parity", parity=2)
+                crossed = crossed_pool.tile([P, 2, UNIT_ROWS], F32, name="crossed")
+                nc.scalar.activation(out=crossed[:, 0, :], in_=pairs[:, :, 1], func=ACT.Copy, scale=minus_sin_t)
+                nc.scalar.activation(out=crossed[:, 1, :], in_=pairs[:, :, 0], func=ACT.Copy, scale=sin_t)
+                rotated = rotated_pool.tile([P, UNIT_ROWS, 2], F32, name="rotated")
+                nc.vector.scalar_tensor_tensor(
+                    out=rotated[:],
+                    in0=pairs,
+                    scalar=cos_t,
+                    in1=crossed[:].rearrange("p parity n -> p n parity"),
+                    op0=ALU.mult,
+                    op1=ALU.add,
+                )
                 nc.sync.dma_start(
                     out=result[first_batch : first_batch + 2, :, first_channel : first_channel + UNIT_ROWS].rearrange(
                         "b t c -> t b c"
                     ),
-                    in_=rotated[:].rearrange("p j i parity -> p j (i parity)"),
+                    in_=rotated[:].rearrange("p (j i) parity -> p j (i parity)", j=2),
                 )
 
         for n in range(LOADS_AHEAD):
@@ -194,11 +191,11 @@ def tile_attention_pa_kernel(tc, x, wq, wk, out_0, out_1):
             transpose_and_quantise(h, x_codes[:, :, tokens_of_unit], x_scales[:, :, tokens_of_unit])
 
         prepared = {}
-        for r in range(ROUNDS + 1):
-            for unit in range(UNITS_PER_ROUND * r, min(UNITS_PER_ROUND * (r + 1), WEIGHT_UNITS)):
+        for step in range(WEIGHT_UNITS + 1):
+            if step < WEIGHT_UNITS:
                 w_codes = weight_mx.tile([P, PASSES, UNIT_ROWS], U32, name="w_codes", align_bytes=64)
                 w_scales = weight_mx.tile([P, PASSES, UNIT_ROWS], U8, name="w_scales", align_bytes=64)
-                prepared[unit] = (w_codes, w_scales)
-                transpose_and_quantise(X_UNITS + unit, w_codes, w_scales)
-            for unit in range(max(UNITS_PER_ROUND * r - LAG, 0), min(UNITS_PER_ROUND * (r + 1) - LAG, WEIGHT_UNITS)):
-                project_and_rotate(unit)
+                prepared[step] = (w_codes, w_scales)
+                transpose_and_quantise(X_UNITS + step, w_codes, w_scales)
+            if step > 0:
+                project_and_rotate(step - 1)

import math
from contextlib import ExitStack

import concourse.mybir as mybir
from concourse.masks import make_identity

F32 = mybir.dt.float32
BF16 = mybir.dt.bfloat16
I32 = mybir.dt.int32
U32 = mybir.dt.uint32
U8 = mybir.dt.uint8
FP8X4 = mybir.dt.float8_e4m3fn_x4
ALU = mybir.AluOpType
ACT = mybir.ActivationFunctionType

P = 128
BATCHES = 4
CHANNELS = 2048
PACK = 4
PASSES = CHANNELS // (P * PACK)
UNIT_ROWS = 2 * P
X_UNITS = BATCHES * P // UNIT_ROWS
UNITS_PER_WEIGHT = CHANNELS // UNIT_ROWS
WEIGHT_UNITS = 2 * UNITS_PER_WEIGHT
LOADS_AHEAD = 8
RAW_BUFFERS = LOADS_AHEAD + 2
TRANSPOSE_BANKS = 4
ACCUMULATOR_BANKS = 4

FLOPS = 2 * (BATCHES * P) * CHANNELS * (2 * CHANNELS)

TWO_PI = 2.0 * math.pi
TWO_PI_HIGH = 6.28125
TWO_PI_MID = int((TWO_PI - TWO_PI_HIGH) * 2**25) / 2**25
TWO_PI_LOW = TWO_PI - TWO_PI_HIGH - TWO_PI_MID
HALF_PI_HIGH = int(0.5 * math.pi * 2**20) / 2**20
HALF_PI_LOW = 0.5 * math.pi - HALF_PI_HIGH
ROUND_TO_WHOLE = 1.5 * 2**23


def position_trig(nc, pool):
    position_int = pool.tile([P, 1], I32, name="position_int")
    nc.gpsimd.iota(position_int[:], pattern=[[0, 1]], base=0, channel_multiplier=1)
    position = pool.tile([P, 1], F32, name="position")
    nc.vector.tensor_copy(out=position[:], in_=position_int[:])

    shifted = pool.tile([P, 1], F32, name="shifted")
    nc.vector.tensor_scalar(
        out=shifted[:], in0=position[:], scalar1=1.0 / TWO_PI, scalar2=ROUND_TO_WHOLE, op0=ALU.mult, op1=ALU.add
    )
    turns = pool.tile([P, 1], F32, name="turns")
    nc.vector.tensor_scalar(out=turns[:], in0=shifted[:], scalar1=ROUND_TO_WHOLE, scalar2=None, op0=ALU.subtract)

    angles = pool.tile([P, 2], F32, name="angles")
    less_high = pool.tile([P, 1], F32, name="less_high")
    less_mid = pool.tile([P, 1], F32, name="less_mid")
    nc.vector.scalar_tensor_tensor(
        out=less_high[:], in0=turns[:], scalar=-TWO_PI_HIGH, in1=position[:], op0=ALU.mult, op1=ALU.add
    )
    nc.vector.scalar_tensor_tensor(
        out=less_mid[:], in0=turns[:], scalar=-TWO_PI_MID, in1=less_high[:], op0=ALU.mult, op1=ALU.add
    )
    nc.vector.scalar_tensor_tensor(
        out=angles[:, 0:1], in0=turns[:], scalar=-TWO_PI_LOW, in1=less_mid[:], op0=ALU.mult, op1=ALU.add
    )
    magnitude = pool.tile([P, 1], F32, name="magnitude")
    nc.vector.scalar_tensor_tensor(
        out=magnitude[:], in0=angles[:, 0:1], scalar=-1.0, in1=angles[:, 0:1], op0=ALU.mult, op1=ALU.max
    )
    nc.vector.tensor_scalar(
        out=angles[:, 1:2],
        in0=magnitude[:],
        scalar1=HALF_PI_HIGH,
        scalar2=HALF_PI_LOW,
        op0=ALU.subtract,
        op1=ALU.subtract,
    )

    sines = pool.tile([P, 2], F32, name="sines")
    nc.scalar.activation(out=sines[:], in_=angles[:], func=ACT.Sin)
    negated = pool.tile([P, 2], F32, name="negated")
    nc.vector.tensor_scalar(out=negated[:], in0=sines[:], scalar1=-1.0, scalar2=None, op0=ALU.mult)
    return sines[:, 0:1], negated[:, 0:1], negated[:, 1:2]


def tile_attention_pa_kernel(tc, x, wq, wk, out_0, out_1):
    nc = tc.nc

    sources = [x[2 * h : 2 * h + 2].rearrange("b t k -> t b k") for h in range(X_UNITS)]
    for weight in (wq, wk):
        for c in range(UNITS_PER_WEIGHT):
            rows = weight[c * UNIT_ROWS : (c + 1) * UNIT_ROWS, :]
            sources.append(rows.rearrange("(j r) k -> r j k", j=2))

    outputs = [out.rearrange("b t h d -> b t (h d)") for out in (out_0, out_1)]

    with ExitStack() as stack:
        const = stack.enter_context(tc.tile_pool(name="const", bufs=1))
        raw_pool = stack.enter_context(tc.tile_pool(name="raw", bufs=RAW_BUFFERS))
        grouped_pool = stack.enter_context(tc.tile_pool(name="grouped", bufs=2 * PASSES))
        weight_mx = stack.enter_context(tc.tile_pool(name="weight_mx", bufs=3))
        crossed_pool = stack.enter_context(tc.tile_pool(name="crossed", bufs=ACCUMULATOR_BANKS))
        rotated_pool = stack.enter_context(tc.tile_pool(name="rotated", bufs=ACCUMULATOR_BANKS + 2))
        transposed_pool = stack.enter_context(tc.psum_pool(name="transposed", bufs=TRANSPOSE_BANKS))
        acc_pool = stack.enter_context(tc.psum_pool(name="acc", bufs=ACCUMULATOR_BANKS))
        stack.enter_context(tc.manual_schedule())

        raw_tiles = {}

        def start_load(n):
            raw = raw_pool.tile([P, 2, CHANNELS], BF16, name="raw")
            nc.sync.dma_start(out=raw[:], in_=sources[n])
            raw_tiles[n] = raw

        def transpose_and_quantise(n, codes, scales):
            if n + LOADS_AHEAD < len(sources):
                start_load(n + LOADS_AHEAD)
            raw_words = raw_tiles[n][:].bitcast(F32)
            grouped_tiles = []
            for g in range(PASSES):
                bank = transposed_pool.tile([P, 2, 2, P], F32, name="bank")
                for plane in range(2):
                    first_word = (2 * g + plane) * P
                    for j in range(2):
                        nc.tensor.transpose(
                            out=bank[:, plane, j, :],
                            in_=raw_words[:, j, first_word : first_word + P],
                            identity=identity[:],
                        )
                grouped = grouped_pool.tile([P, UNIT_ROWS, PACK], BF16, name="grouped", align_bytes=64)
                copy_out = nc.vector.tensor_copy if g == PASSES - 1 else nc.scalar.copy
                copy_out(out=grouped[:].bitcast(F32), in_=bank[:].rearrange("p plane j r -> p (j r) plane"))
                grouped_tiles.append(grouped)
            for g in range(PASSES):
                nc.vector.quantize_mx(
                    out=codes[:, g, :].bitcast(FP8X4),
                    scales=scales[:, g, :],
                    in_=grouped_tiles[g][:].rearrange("p n t -> p (n t)"),
                )

        def project_and_rotate(unit):
            w_codes, w_scales = prepared[unit]
            result = outputs[unit // UNITS_PER_WEIGHT]
            first_channel = (unit % UNITS_PER_WEIGHT) * UNIT_ROWS
            for first_batch in range(0, BATCHES, 2):
                acc = acc_pool.tile([P, 2, UNIT_ROWS], F32, name="acc")
                for j in range(2):
                    tokens = slice((first_batch + j) * P, (first_batch + j + 1) * P)
                    for g in range(PASSES):
                        nc.tensor.matmul_mx(
                            out=acc[:, j, :],
                            lhsT=x_codes[:, g, tokens].bitcast(FP8X4),
                            lhsT_scale=x_scales[:, g, tokens],
                            rhs=w_codes[:, g, :].bitcast(FP8X4),
                            rhs_scale=w_scales[:, g, :],
                            start=(g == 0),
                            stop=(g == PASSES - 1),
                        )
                pairs = acc[:].rearrange("p j (i parity) -> p (j i) parity", parity=2)
                crossed = crossed_pool.tile([P, 2, UNIT_ROWS], F32, name="crossed")
                nc.scalar.activation(out=crossed[:, 0, :], in_=pairs[:, :, 1], func=ACT.Copy, scale=minus_sin_t)
                nc.scalar.activation(out=crossed[:, 1, :], in_=pairs[:, :, 0], func=ACT.Copy, scale=sin_t)
                rotated = rotated_pool.tile([P, UNIT_ROWS, 2], F32, name="rotated")
                nc.vector.scalar_tensor_tensor(
                    out=rotated[:],
                    in0=pairs,
                    scalar=cos_t,
                    in1=crossed[:].rearrange("p parity n -> p n parity"),
                    op0=ALU.mult,
                    op1=ALU.add,
                )
                nc.sync.dma_start(
                    out=result[first_batch : first_batch + 2, :, first_channel : first_channel + UNIT_ROWS].rearrange(
                        "b t c -> t b c"
                    ),
                    in_=rotated[:].rearrange("p (j i) parity -> p j (i parity)", j=2),
                )

        for n in range(LOADS_AHEAD):
            start_load(n)

        identity = const.tile([P, P], F32, name="identity")
        make_identity(nc, identity[:])

        sin_t, minus_sin_t, cos_t = position_trig(nc, const)

        x_codes = const.tile([P, PASSES, BATCHES * P], U32, name="x_codes", align_bytes=64)
        x_scales = const.tile([P, PASSES, BATCHES * P], U8, name="x_scales", align_bytes=64)
        for h in range(X_UNITS):
            tokens_of_unit = slice(h * UNIT_ROWS, (h + 1) * UNIT_ROWS)
            transpose_and_quantise(h, x_codes[:, :, tokens_of_unit], x_scales[:, :, tokens_of_unit])

        prepared = {}
        for step in range(WEIGHT_UNITS + 1):
            if step < WEIGHT_UNITS:
                w_codes = weight_mx.tile([P, PASSES, UNIT_ROWS], U32, name="w_codes", align_bytes=64)
                w_scales = weight_mx.tile([P, PASSES, UNIT_ROWS], U8, name="w_scales", align_bytes=64)
                prepared[step] = (w_codes, w_scales)
                transpose_and_quantise(X_UNITS + step, w_codes, w_scales)
            if step > 0:
                project_and_rotate(step - 1)
